import numpy as np
import ml_dtypes


def mxq(x, axis, fmt="e4m3"):
    dtype, down = {"e4m3": (ml_dtypes.float8_e4m3fn, 7), "e5m2": (ml_dtypes.float8_e5m2, 14)}[fmt]
    v = np.moveaxis(np.asarray(x, np.float32).astype(ml_dtypes.bfloat16).astype(np.float64), axis, -1)
    blocks = v.reshape(v.shape[:-1] + (-1, 32))
    amax = np.abs(blocks).max(-1, keepdims=True)
    byte = np.maximum(np.where(amax > 0, np.frexp(amax)[1] - 1 + 127, 0) - down, 1)
    scale = np.exp2(byte - 127.0)
    codes = (blocks / scale).astype(np.float32).astype(dtype).astype(np.float64)
    return np.moveaxis((codes * scale).reshape(v.shape), -1, axis)


WIDE = False


def mx_kscale(k):
    if not WIDE:
        return np.ones(k)
    levels = np.array([10, -10, 5, -5, 0])
    a = np.random.permutation(np.resize(levels, k // 512 * 4)).reshape(k // 512, 4)
    idx = np.arange(k)
    return np.exp2(a[idx // 512, idx % 128 // 32])


BF16 = ml_dtypes.bfloat16


def bf(x):
    return np.asarray(x, np.float32).astype(BF16)


def f64(x):
    return np.asarray(x).astype(np.float64)


B, D, S, N = 128, 1024, 4, 128
DS = D // S


def sigmoid(v):
    return 1.0 / (1.0 + np.exp(-v))


def setup_inputs():
    s = mx_kscale(D)
    t = np.maximum(1.0 + 2.0 * np.random.standard_normal((B, N, S)), 0.0) + np.maximum(1.0 + 2.0 * np.random.standard_normal((B, N, S)), 0.0)
    return {"a": bf(t * t / (t * t).sum(axis=1, keepdims=True)),
            "vr": bf(np.random.standard_normal((N, S, DS)) * 0.5 * np.sqrt(N) * s.reshape(S, DS)),
            "h": bf(np.random.standard_normal((B, D)) * s),
            "x2g": bf(np.random.standard_normal((B, D))),
            "w_g": bf(np.random.standard_normal((D, D)) / np.sqrt(D) / s),
            "b_g": bf(np.random.standard_normal(D) * 0.3),
            "bg": bf(1.0 + 0.1 * np.random.standard_normal(1))}


def reference(a, vr, h, x2g, w_g, b_g, bg):
    hf = f64(h)
    hh = (f64(a).transpose(2, 0, 1) @ f64(vr).transpose(1, 0, 2)).transpose(1, 0, 2).reshape(B, D)
    h2g = (mxq(hf, 1, "e4m3") @ mxq(f64(w_g), 1, "e4m3").T) + f64(b_g)
    g = sigmoid(f64(x2g) + h2g + f64(bg))
    return g * hh + (1.0 - g) * hf

@@ -1,0 +1,156 @@
+from contextlib import ExitStack
+
+import concourse.mybir as mybir
+from concourse.masks import make_identity
+
+F32 = mybir.dt.float32
+BF16 = mybir.dt.bfloat16
+U32 = mybir.dt.uint32
+U8 = mybir.dt.uint8
+FP8X4 = mybir.dt.float8_e4m3fn_x4
+ADD = mybir.AluOpType.add
+SUBTRACT = mybir.AluOpType.subtract
+MULT = mybir.AluOpType.mult
+SIGMOID = mybir.ActivationFunctionType.Sigmoid
+
+P = 128
+D = 1024
+SLICES = 4
+DS = D // SLICES
+PACK = 4
+K_PASS = P * PACK
+PASSES = D // K_PASS
+HALVES = 2
+ROW_TILES = DS // P
+BIAS_RUN = D // P
+
+FLOPS = 2 * P * D * D + 2 * P * P * D
+
+
+def tile_tpru_pb_s_kernel(tc, a, vr, h, x2g, w_g, b_g, bg, out):
+    nc = tc.nc
+    with ExitStack() as ctx:
+        keep = ctx.enter_context(tc.tile_pool(name="keep", bufs=1))
+        stage = ctx.enter_context(tc.tile_pool(name="stage", bufs=2))
+        flip = ctx.enter_context(tc.psum_pool(name="flip", bufs=4))
+        roles = ctx.enter_context(tc.psum_pool(name="roles", bufs=1))
+        gate = ctx.enter_context(tc.psum_pool(name="gate", bufs=2))
+
+        h_sb = keep.tile([P, D], BF16)
+        nc.sync.dma_start(out=h_sb[:], in_=h)
+        w_sb = []
+        for grp in range(SLICES):
+            w_rows = keep.tile([P, ROW_TILES, D], BF16, name="w_rows%d" % grp)
+            nc.sync.dma_start(
+                out=w_rows[:],
+                in_=w_g[grp * DS : (grp + 1) * DS, :].rearrange("(j p) k -> p j k", p=P),
+            )
+            w_sb.append(w_rows)
+        b_runs = keep.tile([P, BIAS_RUN], BF16)
+        nc.scalar.dma_start(out=b_runs[:], in_=b_g.rearrange("(p m) -> p m", m=BIAS_RUN))
+        bg_bf = keep.tile([P, 1], BF16)
+        nc.scalar.dma_start(out=bg_bf[:], in_=bg.partition_broadcast(P))
+        x_sb = keep.tile([P, D], BF16)
+        nc.scalar.dma_start(out=x_sb[:], in_=x2g)
+        a_sb = keep.tile([P, P, SLICES], BF16)
+        nc.scalar.dma_start(out=a_sb[:], in_=a)
+        vr_sb = keep.tile([P, SLICES, DS], BF16)
+        nc.scalar.dma_start(out=vr_sb[:], in_=vr)
+
+        ident_f32 = keep.tile([P, P], F32)
+        make_identity(nc, ident_f32[:])
+        ident_bf = keep.tile([P, P], BF16)
+        make_identity(nc, ident_bf[:])
+        zero_col = keep.tile([P, 1], F32)
+        nc.vector.memset(zero_col[:], 0.0)
+        half_col = keep.tile([P, 1], F32)
+        nc.scalar.activation(out=half_col[:], in_=zero_col[:], func=SIGMOID)
+
+        h_words = h_sb[:].bitcast(F32)
+        h_flip = flip.tile([P, PASSES, HALVES, P], F32, tag="flip")
+        for c in range(PASSES):
+            for u in range(HALVES):
+                first = (c * HALVES + u) * P
+                nc.tensor.transpose(h_flip[:, c, u, :], h_words[:, first : first + P], ident_f32[:])
+        h_grouped = keep.tile([P, PASSES, P, PACK], BF16, align_bytes=64)
+        nc.scalar.copy(out=h_grouped[:].bitcast(F32), in_=h_flip[:].rearrange("p c u b -> p c b u"))
+        h_codes = keep.tile([P, PASSES * P], U32, align_bytes=64)
+        h_scales = keep.tile([P, PASSES * P], U8, align_bytes=64)
+        nc.vector.quantize_mx(
+            out=h_codes[:].bitcast(FP8X4),
+            scales=h_scales[:],
+            in_=h_grouped[:].rearrange("p c b t -> p (c b t)"),
+        )
+
+        bias_flip = flip.tile([P, BIAS_RUN, P], BF16, tag="flip")
+        for m in range(BIAS_RUN):
+            nc.tensor.transpose(bias_flip[:, m, :], b_runs[:, m : m + 1].to_broadcast([P, P]), ident_bf[:])
+        bg_f32 = keep.tile([P, 1], F32)
+        nc.vector.tensor_copy(out=bg_f32[:], in_=bg_bf[:])
+        pre = keep.tile([P, D], F32)
+        nc.vector.scalar_tensor_tensor(
+            out=pre[:].rearrange("b (p m) -> b p m", m=BIAS_RUN),
+            in0=bias_flip[:].rearrange("b m p -> b p m"),
+            scalar=bg_f32[:, 0:1],
+            in1=x_sb[:].rearrange("b (p m) -> b p m", m=BIAS_RUN),
+            op0=ADD,
+            op1=ADD,
+        )
+
+        a_flip = flip.tile([P, SLICES, P], BF16, tag="flip")
+        for s in range(SLICES):
+            nc.tensor.transpose(a_flip[:, s, :], a_sb[:, :, s], ident_bf[:])
+        a_t = keep.tile([P, SLICES, P], BF16)
+        nc.scalar.copy(out=a_t[:], in_=a_flip[:])
+        diff = keep.tile([P, D], F32)
+        for bank in range(SLICES // 2):
+            hh = roles.tile([P, 2, DS], F32, name="hh%d" % bank)
+            for i in range(2):
+                s = 2 * bank + i
+                nc.tensor.matmul(out=hh[:, i, :], lhsT=a_t[:, s, :], rhs=vr_sb[:, s, :], start=True, stop=True)
+            cols = slice(2 * bank * DS, 2 * (bank + 1) * DS)
+            nc.vector.tensor_tensor(
+                out=diff[:, cols], in0=hh[:].rearrange("b i d -> b (i d)"), in1=h_sb[:, cols], op=SUBTRACT
+            )
+
+        w_codes = keep.tile([P, SLICES, PASSES * DS], U32, align_bytes=64)
+        w_scales = keep.tile([P, SLICES, PASSES * DS], U8, align_bytes=64)
+        z = keep.tile([P, D], F32)
+        g = keep.tile([P, D], F32)
+        blend = keep.tile([P, D], F32)
+        result = keep.tile([P, D], F32)
+        for grp in range(SLICES):
+            w_words = w_sb[grp][:].bitcast(F32)
+            w_grouped = stage.tile([P, PASSES, DS, PACK], BF16, align_bytes=64)
+            w_grouped_words = w_grouped[:].bitcast(F32)
+            for c in range(PASSES):
+                w_flip = flip.tile([P, HALVES, DS], F32, tag="flip")
+                for u in range(HALVES):
+                    first = (c * HALVES + u) * P
+                    for j in range(ROW_TILES):
+                        nc.tensor.transpose(
+                            w_flip[:, u, j * P : (j + 1) * P], w_words[:, j, first : first + P], ident_f32[:]
+                        )
+                nc.scalar.copy(out=w_grouped_words[:, c, :, :], in_=w_flip[:].rearrange("p u o -> p o u"))
+            nc.vector.quantize_mx(
+                out=w_codes[:, grp, :].bitcast(FP8X4),
+                scales=w_scales[:, grp, :],
+                in_=w_grouped[:].rearrange("p c o t -> p (c o t)"),
+            )
+            h2g = gate.tile([P, DS], F32)
+            for c in range(PASSES):
+                nc.tensor.matmul_mx(
+                    out=h2g[:],
+                    lhsT=h_codes[:, c * P : (c + 1) * P].bitcast(FP8X4),
+                    lhsT_scale=h_scales[:, c * P : (c + 1) * P],
+                    rhs=w_codes[:, grp, c * DS : (c + 1) * DS].bitcast(FP8X4),
+                    rhs_scale=w_scales[:, grp, c * DS : (c + 1) * DS],
+                    start=(c == 0),
+                    stop=(c == PASSES - 1),
+                )
+            cols = slice(grp * DS, (grp + 1) * DS)
+            nc.vector.tensor_tensor(out=z[:, cols], in0=h2g[:], in1=pre[:, cols], op=ADD)
+            nc.scalar.activation(out=g[:, cols], in_=z[:, cols], func=SIGMOID)
+            nc.vector.tensor_tensor(out=blend[:, cols], in0=g[:, cols], in1=diff[:, cols], op=MULT)
+            nc.vector.tensor_tensor(out=result[:, cols], in0=blend[:, cols], in1=h_sb[:, cols], op=ADD)
+            nc.sync.dma_start(out=out[:, cols], in_=result[:, cols])

@@ -35,6 +35,7 @@ def tile_tpru_pb_s_kernel(tc, a, vr, h, x2g, w_g, b_g, bg, out):
         flip = ctx.enter_context(tc.psum_pool(name="flip", bufs=4))
         roles = ctx.enter_context(tc.psum_pool(name="roles", bufs=1))
         gate = ctx.enter_context(tc.psum_pool(name="gate", bufs=2))
+        ctx.enter_context(tc.manual_schedule())
 
         h_sb = keep.tile([P, D], BF16)
         nc.sync.dma_start(out=h_sb[:], in_=h)
@@ -74,13 +75,6 @@ def tile_tpru_pb_s_kernel(tc, a, vr, h, x2g, w_g, b_g, bg, out):
                 nc.tensor.transpose(h_flip[:, c, u, :], h_words[:, first : first + P], ident_f32[:])
         h_grouped = keep.tile([P, PASSES, P, PACK], BF16, align_bytes=64)
         nc.scalar.copy(out=h_grouped[:].bitcast(F32), in_=h_flip[:].rearrange("p c u b -> p c b u"))
-        h_codes = keep.tile([P, PASSES * P], U32, align_bytes=64)
-        h_scales = keep.tile([P, PASSES * P], U8, align_bytes=64)
-        nc.vector.quantize_mx(
-            out=h_codes[:].bitcast(FP8X4),
-            scales=h_scales[:],
-            in_=h_grouped[:].rearrange("p c b t -> p (c b t)"),
-        )
 
         bias_flip = flip.tile([P, BIAS_RUN, P], BF16, tag="flip")
         for m in range(BIAS_RUN):
@@ -95,6 +89,13 @@ def tile_tpru_pb_s_kernel(tc, a, vr, h, x2g, w_g, b_g, bg, out):
             in1=x_sb[:].rearrange("b (p m) -> b p m", m=BIAS_RUN),
             op0=ADD,
             op1=ADD,
+        )
+        h_codes = keep.tile([P, PASSES * P], U32, align_bytes=64)
+        h_scales = keep.tile([P, PASSES * P], U8, align_bytes=64)
+        nc.vector.quantize_mx(
+            out=h_codes[:].bitcast(FP8X4),
+            scales=h_scales[:],
+            in_=h_grouped[:].rearrange("p c b t -> p (c b t)"),
         )
 
         a_flip = flip.tile([P, SLICES, P], BF16, tag="flip")
@@ -119,12 +120,13 @@ def tile_tpru_pb_s_kernel(tc, a, vr, h, x2g, w_g, b_g, bg, out):
         g = keep.tile([P, D], F32)
         blend = keep.tile([P, D], F32)
         result = keep.tile([P, D], F32)
-        for grp in range(SLICES):
+
+        def quantise_group(grp):
             w_words = w_sb[grp][:].bitcast(F32)
-            w_grouped = stage.tile([P, PASSES, DS, PACK], BF16, align_bytes=64)
+            w_grouped = stage.tile([P, PASSES, DS, PACK], BF16, align_bytes=64, name="w_grouped")
             w_grouped_words = w_grouped[:].bitcast(F32)
             for c in range(PASSES):
-                w_flip = flip.tile([P, HALVES, DS], F32, tag="flip")
+                w_flip = flip.tile([P, HALVES, DS], F32, tag="flip", name="w_flip")
                 for u in range(HALVES):
                     first = (c * HALVES + u) * P
                     for j in range(ROW_TILES):
@@ -137,7 +139,10 @@ def tile_tpru_pb_s_kernel(tc, a, vr, h, x2g, w_g, b_g, bg, out):
                 scales=w_scales[:, grp, :],
                 in_=w_grouped[:].rearrange("p c o t -> p (c o t)"),
             )
-            h2g = gate.tile([P, DS], F32)
+
+        def multiply_group(grp):
+            cols = slice(grp * DS, (grp + 1) * DS)
+            h2g = gate.tile([P, DS], F32, name="h2g")
             for c in range(PASSES):
                 nc.tensor.matmul_mx(
                     out=h2g[:],
@@ -148,9 +153,19 @@ def tile_tpru_pb_s_kernel(tc, a, vr, h, x2g, w_g, b_g, bg, out):
                     start=(c == 0),
                     stop=(c == PASSES - 1),
                 )
-            cols = slice(grp * DS, (grp + 1) * DS)
             nc.vector.tensor_tensor(out=z[:, cols], in0=h2g[:], in1=pre[:, cols], op=ADD)
+
+        def blend_group(grp):
+            cols = slice(grp * DS, (grp + 1) * DS)
             nc.scalar.activation(out=g[:, cols], in_=z[:, cols], func=SIGMOID)
             nc.vector.tensor_tensor(out=blend[:, cols], in0=g[:, cols], in1=diff[:, cols], op=MULT)
             nc.vector.tensor_tensor(out=result[:, cols], in0=blend[:, cols], in1=h_sb[:, cols], op=ADD)
             nc.sync.dma_start(out=out[:, cols], in_=result[:, cols])
+
+        for rnd in range(SLICES + 2):
+            if rnd < SLICES:
+                quantise_group(rnd)
+            if 0 <= rnd - 1 < SLICES:
+                multiply_group(rnd - 1)
+            if 0 <= rnd - 2:
+                blend_group(rnd - 2)

@@ -23,6 +23,8 @@ PASSES = D // K_PASS
 HALVES = 2
 ROW_TILES = DS // P
 BIAS_RUN = D // P
+IDLE_COLS = 256
+WARM_PASSES = 12
 
 FLOPS = 2 * P * D * D + 2 * P * P * D
 
@@ -57,6 +59,27 @@ def tile_tpru_pb_s_kernel(tc, a, vr, h, x2g, w_g, b_g, bg, out):
         nc.scalar.dma_start(out=a_sb[:], in_=a)
         vr_sb = keep.tile([P, SLICES, DS], BF16)
         nc.scalar.dma_start(out=vr_sb[:], in_=vr)
+
+        idle_values = keep.tile([P, IDLE_COLS * PACK], BF16, align_bytes=64)
+        nc.vector.memset(idle_values[:], 1.0)
+        idle_codes = keep.tile([P, IDLE_COLS], U32, align_bytes=64)
+        idle_scales = keep.tile([P, IDLE_COLS], U8, align_bytes=64)
+        nc.vector.quantize_mx(out=idle_codes[:].bitcast(FP8X4), scales=idle_scales[:], in_=idle_values[:])
+
+        def idle_passes(spare, count):
+            for i in range(count):
+                nc.tensor.matmul_mx(
+                    out=spare[:],
+                    lhsT=idle_codes[:, 0:P].bitcast(FP8X4),
+                    lhsT_scale=idle_scales[:, 0:P],
+                    rhs=idle_codes[:].bitcast(FP8X4),
+                    rhs_scale=idle_scales[:],
+                    start=True,
+                    stop=True,
+                )
+
+        spare_early = roles.tile([P, IDLE_COLS], F32, tag="hh0")
+        idle_passes(spare_early, WARM_PASSES)
 
         ident_f32 = keep.tile([P, P], F32)
         make_identity(nc, ident_f32[:])
@@ -103,9 +126,10 @@ def tile_tpru_pb_s_kernel(tc, a, vr, h, x2g, w_g, b_g, bg, out):
             nc.tensor.transpose(a_flip[:, s, :], a_sb[:, :, s], ident_bf[:])
         a_t = keep.tile([P, SLICES, P], BF16)
         nc.scalar.copy(out=a_t[:], in_=a_flip[:])
+        idle_passes(spare_early, 4)
         diff = keep.tile([P, D], F32)
         for bank in range(SLICES // 2):
-            hh = roles.tile([P, 2, DS], F32, name="hh%d" % bank)
+            hh = roles.tile([P, 2, DS], F32, tag="hh%d" % bank, name="hh%d" % bank)
             for i in range(2):
                 s = 2 * bank + i
                 nc.tensor.matmul(out=hh[:, i, :], lhsT=a_t[:, s, :], rhs=vr_sb[:, s, :], start=True, stop=True)
@@ -113,6 +137,8 @@ def tile_tpru_pb_s_kernel(tc, a, vr, h, x2g, w_g, b_g, bg, out):
             nc.vector.tensor_tensor(
                 out=diff[:, cols], in0=hh[:].rearrange("b i d -> b (i d)"), in1=h_sb[:, cols], op=SUBTRACT
             )
+
+        spare_late = roles.tile([P, IDLE_COLS], F32, tag="hh0")
 
         w_codes = keep.tile([P, SLICES, PASSES * DS], U32, align_bytes=64)
         w_scales = keep.tile([P, SLICES, PASSES * DS], U8, align_bytes=64)
@@ -167,5 +193,7 @@ def tile_tpru_pb_s_kernel(tc, a, vr, h, x2g, w_g, b_g, bg, out):
                 quantise_group(rnd)
             if 0 <= rnd - 1 < SLICES:
                 multiply_group(rnd - 1)
+            if rnd < SLICES:
+                idle_passes(spare_late, 2)
             if 0 <= rnd - 2:
                 blend_group(rnd - 2)

@@ -21,10 +21,10 @@ PACK = 4
 K_PASS = P * PACK
 PASSES = D // K_PASS
 HALVES = 2
-ROW_TILES = DS // P
+GROUPS = D // P
 BIAS_RUN = D // P
-IDLE_COLS = 256
-WARM_PASSES = 12
+MULTIPLY_LAG = 2
+BLEND_LAG = 3
 
 FLOPS = 2 * P * D * D + 2 * P * P * D
 
@@ -33,71 +33,37 @@ def tile_tpru_pb_s_kernel(tc, a, vr, h, x2g, w_g, b_g, bg, out):
     nc = tc.nc
     with ExitStack() as ctx:
         keep = ctx.enter_context(tc.tile_pool(name="keep", bufs=1))
-        stage = ctx.enter_context(tc.tile_pool(name="stage", bufs=2))
+        stage = ctx.enter_context(tc.tile_pool(name="stage", bufs=3))
         flip = ctx.enter_context(tc.psum_pool(name="flip", bufs=4))
         roles = ctx.enter_context(tc.psum_pool(name="roles", bufs=1))
         gate = ctx.enter_context(tc.psum_pool(name="gate", bufs=2))
-        ctx.enter_context(tc.manual_schedule())
 
+        b_runs = keep.tile([P, BIAS_RUN], BF16)
+        nc.sync.dma_start(out=b_runs[:], in_=b_g.rearrange("(p m) -> p m", m=BIAS_RUN))
+        bg_bf = keep.tile([P, 1], BF16)
+        nc.sync.dma_start(out=bg_bf[:], in_=bg.partition_broadcast(P))
+        x_sb = keep.tile([P, D], BF16)
+        nc.sync.dma_start(out=x_sb[:], in_=x2g)
         h_sb = keep.tile([P, D], BF16)
         nc.sync.dma_start(out=h_sb[:], in_=h)
-        w_sb = []
-        for grp in range(SLICES):
-            w_rows = keep.tile([P, ROW_TILES, D], BF16, name="w_rows%d" % grp)
-            nc.sync.dma_start(
-                out=w_rows[:],
-                in_=w_g[grp * DS : (grp + 1) * DS, :].rearrange("(j p) k -> p j k", p=P),
-            )
-            w_sb.append(w_rows)
-        b_runs = keep.tile([P, BIAS_RUN], BF16)
-        nc.scalar.dma_start(out=b_runs[:], in_=b_g.rearrange("(p m) -> p m", m=BIAS_RUN))
-        bg_bf = keep.tile([P, 1], BF16)
-        nc.scalar.dma_start(out=bg_bf[:], in_=bg.partition_broadcast(P))
-        x_sb = keep.tile([P, D], BF16)
-        nc.scalar.dma_start(out=x_sb[:], in_=x2g)
         a_sb = keep.tile([P, P, SLICES], BF16)
-        nc.scalar.dma_start(out=a_sb[:], in_=a)
+        nc.sync.dma_start(out=a_sb[:], in_=a)
         vr_sb = keep.tile([P, SLICES, DS], BF16)
-        nc.scalar.dma_start(out=vr_sb[:], in_=vr)
+        nc.sync.dma_start(out=vr_sb[:], in_=vr)
+        w_sb = []
+        for grp in range(GROUPS):
+            w_rows = keep.tile([P, D], BF16, name="w_rows%d" % grp)
+            nc.sync.dma_start(out=w_rows[:], in_=w_g[grp * P : (grp + 1) * P, :])
+            w_sb.append(w_rows)
 
-        idle_values = keep.tile([P, IDLE_COLS * PACK], BF16, align_bytes=64)
-        nc.vector.memset(idle_values[:], 1.0)
-        idle_codes = keep.tile([P, IDLE_COLS], U32, align_bytes=64)
-        idle_scales = keep.tile([P, IDLE_COLS], U8, align_bytes=64)
-        nc.vector.quantize_mx(out=idle_codes[:].bitcast(FP8X4), scales=idle_scales[:], in_=idle_values[:])
-
-        def idle_passes(spare, count):
-            for i in range(count):
-                nc.tensor.matmul_mx(
-                    out=spare[:],
-                    lhsT=idle_codes[:, 0:P].bitcast(FP8X4),
-                    lhsT_scale=idle_scales[:, 0:P],
-                    rhs=idle_codes[:].bitcast(FP8X4),
-                    rhs_scale=idle_scales[:],
-                    start=True,
-                    stop=True,
-                )
-
-        spare_early = roles.tile([P, IDLE_COLS], F32, tag="hh0")
-        idle_passes(spare_early, WARM_PASSES)
-
-        ident_f32 = keep.tile([P, P], F32)
-        make_identity(nc, ident_f32[:])
         ident_bf = keep.tile([P, P], BF16)
         make_identity(nc, ident_bf[:])
+        ident_f32 = keep.tile([P, P], F32)
+        make_identity(nc, ident_f32[:])
         zero_col = keep.tile([P, 1], F32)
         nc.vector.memset(zero_col[:], 0.0)
         half_col = keep.tile([P, 1], F32)
         nc.scalar.activation(out=half_col[:], in_=zero_col[:], func=SIGMOID)
-
-        h_words = h_sb[:].bitcast(F32)
-        h_flip = flip.tile([P, PASSES, HALVES, P], F32, tag="flip")
-        for c in range(PASSES):
-            for u in range(HALVES):
-                first = (c * HALVES + u) * P
-                nc.tensor.transpose(h_flip[:, c, u, :], h_words[:, first : first + P], ident_f32[:])
-        h_grouped = keep.tile([P, PASSES, P, PACK], BF16, align_bytes=64)
-        nc.scalar.copy(out=h_grouped[:].bitcast(F32), in_=h_flip[:].rearrange("p c u b -> p c b u"))
 
         bias_flip = flip.tile([P, BIAS_RUN, P], BF16, tag="flip")
         for m in range(BIAS_RUN):
@@ -113,6 +79,15 @@ def tile_tpru_pb_s_kernel(tc, a, vr, h, x2g, w_g, b_g, bg, out):
             op0=ADD,
             op1=ADD,
         )
+
+        h_words = h_sb[:].bitcast(F32)
+        h_flip = flip.tile([P, PASSES, HALVES, P], F32, tag="flip")
+        for c in range(PASSES):
+            for u in range(HALVES):
+                first = (c * HALVES + u) * P
+                nc.tensor.transpose(h_flip[:, c, u, :], h_words[:, first : first + P], ident_f32[:])
+        h_grouped = keep.tile([P, PASSES, P, PACK], BF16, align_bytes=64)
+        nc.scalar.copy(out=h_grouped[:].bitcast(F32), in_=h_flip[:].rearrange("p c u b -> p c b u"))
         h_codes = keep.tile([P, PASSES * P], U32, align_bytes=64)
         h_scales = keep.tile([P, PASSES * P], U8, align_bytes=64)
         nc.vector.quantize_mx(
@@ -126,10 +101,9 @@ def tile_tpru_pb_s_kernel(tc, a, vr, h, x2g, w_g, b_g, bg, out):
             nc.tensor.transpose(a_flip[:, s, :], a_sb[:, :, s], ident_bf[:])
         a_t = keep.tile([P, SLICES, P], BF16)
         nc.scalar.copy(out=a_t[:], in_=a_flip[:])
-        idle_passes(spare_early, 4)
         diff = keep.tile([P, D], F32)
         for bank in range(SLICES // 2):
-            hh = roles.tile([P, 2, DS], F32, tag="hh%d" % bank, name="hh%d" % bank)
+            hh = roles.tile([P, 2, DS], F32, name="hh%d" % bank)
             for i in range(2):
                 s = 2 * bank + i
                 nc.tensor.matmul(out=hh[:, i, :], lhsT=a_t[:, s, :], rhs=vr_sb[:, s, :], start=True, stop=True)
@@ -138,10 +112,8 @@ def tile_tpru_pb_s_kernel(tc, a, vr, h, x2g, w_g, b_g, bg, out):
                 out=diff[:, cols], in0=hh[:].rearrange("b i d -> b (i d)"), in1=h_sb[:, cols], op=SUBTRACT
             )
 
-        spare_late = roles.tile([P, IDLE_COLS], F32, tag="hh0")
-
-        w_codes = keep.tile([P, SLICES, PASSES * DS], U32, align_bytes=64)
-        w_scales = keep.tile([P, SLICES, PASSES * DS], U8, align_bytes=64)
+        w_codes = keep.tile([P, GROUPS, PASSES * P], U32, align_bytes=64)
+        w_scales = keep.tile([P, GROUPS, PASSES * P], U8, align_bytes=64)
         z = keep.tile([P, D], F32)
         g = keep.tile([P, D], F32)
         blend = keep.tile([P, D], F32)
@@ -149,17 +121,13 @@ def tile_tpru_pb_s_kernel(tc, a, vr, h, x2g, w_g, b_g, bg, out):
 
         def quantise_group(grp):
             w_words = w_sb[grp][:].bitcast(F32)
-            w_grouped = stage.tile([P, PASSES, DS, PACK], BF16, align_bytes=64, name="w_grouped")
-            w_grouped_words = w_grouped[:].bitcast(F32)
+            w_flip = flip.tile([P, PASSES, HALVES, P], F32, tag="flip", name="w_flip")
             for c in range(PASSES):
-                w_flip = flip.tile([P, HALVES, DS], F32, tag="flip", name="w_flip")
                 for u in range(HALVES):
                     first = (c * HALVES + u) * P
-                    for j in range(ROW_TILES):
-                        nc.tensor.transpose(
-                            w_flip[:, u, j * P : (j + 1) * P], w_words[:, j, first : first + P], ident_f32[:]
-                        )
-                nc.scalar.copy(out=w_grouped_words[:, c, :, :], in_=w_flip[:].rearrange("p u o -> p o u"))
+                    nc.tensor.transpose(w_flip[:, c, u, :], w_words[:, first : first + P], ident_f32[:])
+            w_grouped = stage.tile([P, PASSES, P, PACK], BF16, align_bytes=64, name="w_grouped")
+            nc.scalar.copy(out=w_grouped[:].bitcast(F32), in_=w_flip[:].rearrange("p c u o -> p c o u"))
             nc.vector.quantize_mx(
                 out=w_codes[:, grp, :].bitcast(FP8X4),
                 scales=w_scales[:, grp, :],
@@ -167,33 +135,32 @@ def tile_tpru_pb_s_kernel(tc, a, vr, h, x2g, w_g, b_g, bg, out):
             )
 
         def multiply_group(grp):
-            cols = slice(grp * DS, (grp + 1) * DS)
-            h2g = gate.tile([P, DS], F32, name="h2g")
+            cols = slice(grp * P, (grp + 1) * P)
+            h2g = gate.tile([P, P], F32, name="h2g")
             for c in range(PASSES):
                 nc.tensor.matmul_mx(
                     out=h2g[:],
                     lhsT=h_codes[:, c * P : (c + 1) * P].bitcast(FP8X4),
                     lhsT_scale=h_scales[:, c * P : (c + 1) * P],
-                    rhs=w_codes[:, grp, c * DS : (c + 1) * DS].bitcast(FP8X4),
-                    rhs_scale=w_scales[:, grp, c * DS : (c + 1) * DS],
+                    rhs=w_codes[:, grp, c * P : (c + 1) * P].bitcast(FP8X4),
+                    rhs_scale=w_scales[:, grp, c * P : (c + 1) * P],
                     start=(c == 0),
                     stop=(c == PASSES - 1),
                 )
             nc.vector.tensor_tensor(out=z[:, cols], in0=h2g[:], in1=pre[:, cols], op=ADD)
 
         def blend_group(grp):
-            cols = slice(grp * DS, (grp + 1) * DS)
+            cols = slice(grp * P, (grp + 1) * P)
             nc.scalar.activation(out=g[:, cols], in_=z[:, cols], func=SIGMOID)
-            nc.vector.tensor_tensor(out=blend[:, cols], in0=g[:, cols], in1=diff[:, cols], op=MULT)
-            nc.vector.tensor_tensor(out=result[:, cols], in0=blend[:, cols], in1=h_sb[:, cols], op=ADD)
+            blender = nc.gpsimd if grp < GROUPS // 2 else nc.vector
+            blender.tensor_tensor(out=blend[:, cols], in0=g[:, cols], in1=diff[:, cols], op=MULT)
+            blender.tensor_tensor(out=result[:, cols], in0=blend[:, cols], in1=h_sb[:, cols], op=ADD)
             nc.sync.dma_start(out=out[:, cols], in_=result[:, cols])
 
-        for rnd in range(SLICES + 2):
-            if rnd < SLICES:
+        for rnd in range(GROUPS + BLEND_LAG):
+            if rnd < GROUPS:
                 quantise_group(rnd)
-            if 0 <= rnd - 1 < SLICES:
-                multiply_group(rnd - 1)
-            if rnd < SLICES:
-                idle_passes(spare_late, 2)
-            if 0 <= rnd - 2:
-                blend_group(rnd - 2)
+            if 0 <= rnd - MULTIPLY_LAG < GROUPS:
+                multiply_group(rnd - MULTIPLY_LAG)
+            if 0 <= rnd - BLEND_LAG:
+                blend_group(rnd - BLEND_LAG)

@@ -23,6 +23,7 @@ PASSES = D // K_PASS
 HALVES = 2
 GROUPS = D // P
 BIAS_RUN = D // P
+WARM_PASSES = 16
 MULTIPLY_LAG = 2
 BLEND_LAG = 3
 
@@ -55,6 +56,23 @@ def tile_tpru_pb_s_kernel(tc, a, vr, h, x2g, w_g, b_g, bg, out):
             w_rows = keep.tile([P, D], BF16, name="w_rows%d" % grp)
             nc.sync.dma_start(out=w_rows[:], in_=w_g[grp * P : (grp + 1) * P, :])
             w_sb.append(w_rows)
+
+        idle_values = keep.tile([P, P * PACK], BF16, align_bytes=64)
+        nc.vector.memset(idle_values[:], 1.0)
+        idle_codes = keep.tile([P, P], U32, align_bytes=64)
+        idle_scales = keep.tile([P, P], U8, align_bytes=64)
+        nc.vector.quantize_mx(out=idle_codes[:].bitcast(FP8X4), scales=idle_scales[:], in_=idle_values[:])
+        spare_early = roles.tile([P, P], F32, tag="hh0")
+        for i in range(WARM_PASSES):
+            nc.tensor.matmul_mx(
+                out=spare_early[:],
+                lhsT=idle_codes[:].bitcast(FP8X4),
+                lhsT_scale=idle_scales[:],
+                rhs=idle_codes[:].bitcast(FP8X4),
+                rhs_scale=idle_scales[:],
+                start=True,
+                stop=True,
+            )
 
         ident_bf = keep.tile([P, P], BF16)
         make_identity(nc, ident_bf[:])
@@ -103,7 +121,7 @@ def tile_tpru_pb_s_kernel(tc, a, vr, h, x2g, w_g, b_g, bg, out):
         nc.scalar.copy(out=a_t[:], in_=a_flip[:])
         diff = keep.tile([P, D], F32)
         for bank in range(SLICES // 2):
-            hh = roles.tile([P, 2, DS], F32, name="hh%d" % bank)
+            hh = roles.tile([P, 2, DS], F32, tag="hh%d" % bank, name="hh%d" % bank)
             for i in range(2):
                 s = 2 * bank + i
                 nc.tensor.matmul(out=hh[:, i, :], lhsT=a_t[:, s, :], rhs=vr_sb[:, s, :], start=True, stop=True)
@@ -111,6 +129,8 @@ def tile_tpru_pb_s_kernel(tc, a, vr, h, x2g, w_g, b_g, bg, out):
             nc.vector.tensor_tensor(
                 out=diff[:, cols], in0=hh[:].rearrange("b i d -> b (i d)"), in1=h_sb[:, cols], op=SUBTRACT
             )
+
+        spare_late = roles.tile([P, P], F32, tag="hh0")
 
         w_codes = keep.tile([P, GROUPS, PASSES * P], U32, align_bytes=64)
         w_scales = keep.tile([P, GROUPS, PASSES * P], U8, align_bytes=64)
@@ -147,6 +167,16 @@ def tile_tpru_pb_s_kernel(tc, a, vr, h, x2g, w_g, b_g, bg, out):
                     start=(c == 0),
                     stop=(c == PASSES - 1),
                 )
+            last = PASSES - 1
+            nc.tensor.matmul_mx(
+                out=spare_late[:],
+                lhsT=h_codes[:, last * P : (last + 1) * P].bitcast(FP8X4),
+                lhsT_scale=h_scales[:, last * P : (last + 1) * P],
+                rhs=w_codes[:, grp, last * P : (last + 1) * P].bitcast(FP8X4),
+                rhs_scale=w_scales[:, grp, last * P : (last + 1) * P],
+                start=True,
+                stop=True,
+            )
             nc.vector.tensor_tensor(out=z[:, cols], in0=h2g[:], in1=pre[:, cols], op=ADD)
 
         def blend_group(grp):

@@ -23,9 +23,10 @@ PASSES = D // K_PASS
 HALVES = 2
 GROUPS = D // P
 BIAS_RUN = D // P
-WARM_PASSES = 16
-MULTIPLY_LAG = 2
-BLEND_LAG = 3
+RUN = 2
+ROUNDS = GROUPS // RUN
+MULTIPLY_LAG = 1
+BLEND_LAG = 2
 
 FLOPS = 2 * P * D * D + 2 * P * P * D
 
@@ -56,23 +57,6 @@ def tile_tpru_pb_s_kernel(tc, a, vr, h, x2g, w_g, b_g, bg, out):
             w_rows = keep.tile([P, D], BF16, name="w_rows%d" % grp)
             nc.sync.dma_start(out=w_rows[:], in_=w_g[grp * P : (grp + 1) * P, :])
             w_sb.append(w_rows)
-
-        idle_values = keep.tile([P, P * PACK], BF16, align_bytes=64)
-        nc.vector.memset(idle_values[:], 1.0)
-        idle_codes = keep.tile([P, P], U32, align_bytes=64)
-        idle_scales = keep.tile([P, P], U8, align_bytes=64)
-        nc.vector.quantize_mx(out=idle_codes[:].bitcast(FP8X4), scales=idle_scales[:], in_=idle_values[:])
-        spare_early = roles.tile([P, P], F32, tag="hh0")
-        for i in range(WARM_PASSES):
-            nc.tensor.matmul_mx(
-                out=spare_early[:],
-                lhsT=idle_codes[:].bitcast(FP8X4),
-                lhsT_scale=idle_scales[:],
-                rhs=idle_codes[:].bitcast(FP8X4),
-                rhs_scale=idle_scales[:],
-                start=True,
-                stop=True,
-            )
 
         ident_bf = keep.tile([P, P], BF16)
         make_identity(nc, ident_bf[:])
@@ -121,7 +105,7 @@ def tile_tpru_pb_s_kernel(tc, a, vr, h, x2g, w_g, b_g, bg, out):
         nc.scalar.copy(out=a_t[:], in_=a_flip[:])
         diff = keep.tile([P, D], F32)
         for bank in range(SLICES // 2):
-            hh = roles.tile([P, 2, DS], F32, tag="hh%d" % bank, name="hh%d" % bank)
+            hh = roles.tile([P, 2, DS], F32, name="hh%d" % bank)
             for i in range(2):
                 s = 2 * bank + i
                 nc.tensor.matmul(out=hh[:, i, :], lhsT=a_t[:, s, :], rhs=vr_sb[:, s, :], start=True, stop=True)
@@ -129,8 +113,6 @@ def tile_tpru_pb_s_kernel(tc, a, vr, h, x2g, w_g, b_g, bg, out):
             nc.vector.tensor_tensor(
                 out=diff[:, cols], in0=hh[:].rearrange("b i d -> b (i d)"), in1=h_sb[:, cols], op=SUBTRACT
             )
-
-        spare_late = roles.tile([P, P], F32, tag="hh0")
 
         w_codes = keep.tile([P, GROUPS, PASSES * P], U32, align_bytes=64)
         w_scales = keep.tile([P, GROUPS, PASSES * P], U8, align_bytes=64)
@@ -167,16 +149,6 @@ def tile_tpru_pb_s_kernel(tc, a, vr, h, x2g, w_g, b_g, bg, out):
                     start=(c == 0),
                     stop=(c == PASSES - 1),
                 )
-            last = PASSES - 1
-            nc.tensor.matmul_mx(
-                out=spare_late[:],
-                lhsT=h_codes[:, last * P : (last + 1) * P].bitcast(FP8X4),
-                lhsT_scale=h_scales[:, last * P : (last + 1) * P],
-                rhs=w_codes[:, grp, last * P : (last + 1) * P].bitcast(FP8X4),
-                rhs_scale=w_scales[:, grp, last * P : (last + 1) * P],
-                start=True,
-                stop=True,
-            )
             nc.vector.tensor_tensor(out=z[:, cols], in0=h2g[:], in1=pre[:, cols], op=ADD)
 
         def blend_group(grp):
@@ -187,10 +159,13 @@ def tile_tpru_pb_s_kernel(tc, a, vr, h, x2g, w_g, b_g, bg, out):
             blender.tensor_tensor(out=result[:, cols], in0=blend[:, cols], in1=h_sb[:, cols], op=ADD)
             nc.sync.dma_start(out=out[:, cols], in_=result[:, cols])
 
-        for rnd in range(GROUPS + BLEND_LAG):
-            if rnd < GROUPS:
-                quantise_group(rnd)
-            if 0 <= rnd - MULTIPLY_LAG < GROUPS:
-                multiply_group(rnd - MULTIPLY_LAG)
-            if 0 <= rnd - BLEND_LAG:
-                blend_group(rnd - BLEND_LAG)
+        for rnd in range(ROUNDS + BLEND_LAG):
+            for i in range(RUN):
+                if rnd < ROUNDS:
+                    quantise_group(rnd * RUN + i)
+            for i in range(RUN):
+                if 0 <= rnd - MULTIPLY_LAG < ROUNDS:
+                    multiply_group((rnd - MULTIPLY_LAG) * RUN + i)
+            for i in range(RUN):
+                if 0 <= rnd - BLEND_LAG:
+                    blend_group((rnd - BLEND_LAG) * RUN + i)

@@ -154,9 +154,8 @@ def tile_tpru_pb_s_kernel(tc, a, vr, h, x2g, w_g, b_g, bg, out):
         def blend_group(grp):
             cols = slice(grp * P, (grp + 1) * P)
             nc.scalar.activation(out=g[:, cols], in_=z[:, cols], func=SIGMOID)
-            blender = nc.gpsimd if grp < GROUPS // 2 else nc.vector
-            blender.tensor_tensor(out=blend[:, cols], in0=g[:, cols], in1=diff[:, cols], op=MULT)
-            blender.tensor_tensor(out=result[:, cols], in0=blend[:, cols], in1=h_sb[:, cols], op=ADD)
+            nc.vector.tensor_tensor(out=blend[:, cols], in0=g[:, cols], in1=diff[:, cols], op=MULT)
+            nc.vector.tensor_tensor(out=result[:, cols], in0=blend[:, cols], in1=h_sb[:, cols], op=ADD)
             nc.sync.dma_start(out=out[:, cols], in_=result[:, cols])
 
         for rnd in range(ROUNDS + BLEND_LAG):

from contextlib import ExitStack

import concourse.mybir as mybir
from concourse.masks import make_identity

F32 = mybir.dt.float32
BF16 = mybir.dt.bfloat16
U32 = mybir.dt.uint32
U8 = mybir.dt.uint8
FP8X4 = mybir.dt.float8_e4m3fn_x4
ADD = mybir.AluOpType.add
SUBTRACT = mybir.AluOpType.subtract
MULT = mybir.AluOpType.mult
SIGMOID = mybir.ActivationFunctionType.Sigmoid

P = 128
D = 1024
SLICES = 4
DS = D // SLICES
PACK = 4
K_PASS = P * PACK
PASSES = D // K_PASS
HALVES = 2
GROUPS = D // P
BIAS_RUN = D // P
RUN = 2
ROUNDS = GROUPS // RUN
MULTIPLY_LAG = 1
BLEND_LAG = 2

FLOPS = 2 * P * D * D + 2 * P * P * D


def tile_tpru_pb_s_kernel(tc, a, vr, h, x2g, w_g, b_g, bg, out):
    nc = tc.nc
    with ExitStack() as ctx:
        keep = ctx.enter_context(tc.tile_pool(name="keep", bufs=1))
        stage = ctx.enter_context(tc.tile_pool(name="stage", bufs=3))
        flip = ctx.enter_context(tc.psum_pool(name="flip", bufs=4))
        roles = ctx.enter_context(tc.psum_pool(name="roles", bufs=1))
        gate = ctx.enter_context(tc.psum_pool(name="gate", bufs=2))

        b_runs = keep.tile([P, BIAS_RUN], BF16)
        nc.sync.dma_start(out=b_runs[:], in_=b_g.rearrange("(p m) -> p m", m=BIAS_RUN))
        bg_bf = keep.tile([P, 1], BF16)
        nc.sync.dma_start(out=bg_bf[:], in_=bg.partition_broadcast(P))
        x_sb = keep.tile([P, D], BF16)
        nc.sync.dma_start(out=x_sb[:], in_=x2g)
        h_sb = keep.tile([P, D], BF16)
        nc.sync.dma_start(out=h_sb[:], in_=h)
        a_sb = keep.tile([P, P, SLICES], BF16)
        nc.sync.dma_start(out=a_sb[:], in_=a)
        vr_sb = keep.tile([P, SLICES, DS], BF16)
        nc.sync.dma_start(out=vr_sb[:], in_=vr)
        w_sb = []
        for grp in range(GROUPS):
            w_rows = keep.tile([P, D], BF16, name="w_rows%d" % grp)
            nc.sync.dma_start(out=w_rows[:], in_=w_g[grp * P : (grp + 1) * P, :])
            w_sb.append(w_rows)

        ident_bf = keep.tile([P, P], BF16)
        make_identity(nc, ident_bf[:])
        ident_f32 = keep.tile([P, P], F32)
        make_identity(nc, ident_f32[:])
        zero_col = keep.tile([P, 1], F32)
        nc.vector.memset(zero_col[:], 0.0)
        half_col = keep.tile([P, 1], F32)
        nc.scalar.activation(out=half_col[:], in_=zero_col[:], func=SIGMOID)

        bias_flip = flip.tile([P, BIAS_RUN, P], BF16, tag="flip")
        for m in range(BIAS_RUN):
            nc.tensor.transpose(bias_flip[:, m, :], b_runs[:, m : m + 1].to_broadcast([P, P]), ident_bf[:])
        bg_f32 = keep.tile([P, 1], F32)
        nc.vector.tensor_copy(out=bg_f32[:], in_=bg_bf[:])
        pre = keep.tile([P, D], F32)
        nc.vector.scalar_tensor_tensor(
            out=pre[:].rearrange("b (p m) -> b p m", m=BIAS_RUN),
            in0=bias_flip[:].rearrange("b m p -> b p m"),
            scalar=bg_f32[:, 0:1],
            in1=x_sb[:].rearrange("b (p m) -> b p m", m=BIAS_RUN),
            op0=ADD,
            op1=ADD,
        )

        h_words = h_sb[:].bitcast(F32)
        h_flip = flip.tile([P, PASSES, HALVES, P], F32, tag="flip")
        for c in range(PASSES):
            for u in range(HALVES):
                first = (c * HALVES + u) * P
                nc.tensor.transpose(h_flip[:, c, u, :], h_words[:, first : first + P], ident_f32[:])
        h_grouped = keep.tile([P, PASSES, P, PACK], BF16, align_bytes=64)
        nc.scalar.copy(out=h_grouped[:].bitcast(F32), in_=h_flip[:].rearrange("p c u b -> p c b u"))
        h_codes = keep.tile([P, PASSES * P], U32, align_bytes=64)
        h_scales = keep.tile([P, PASSES * P], U8, align_bytes=64)
        nc.vector.quantize_mx(
            out=h_codes[:].bitcast(FP8X4),
            scales=h_scales[:],
            in_=h_grouped[:].rearrange("p c b t -> p (c b t)"),
        )

        a_flip = flip.tile([P, SLICES, P], BF16, tag="flip")
        for s in range(SLICES):
            nc.tensor.transpose(a_flip[:, s, :], a_sb[:, :, s], ident_bf[:])
        a_t = keep.tile([P, SLICES, P], BF16)
        nc.scalar.copy(out=a_t[:], in_=a_flip[:])
        diff = keep.tile([P, D], F32)
        for bank in range(SLICES // 2):
            hh = roles.tile([P, 2, DS], F32, name="hh%d" % bank)
            for i in range(2):
                s = 2 * bank + i
                nc.tensor.matmul(out=hh[:, i, :], lhsT=a_t[:, s, :], rhs=vr_sb[:, s, :], start=True, stop=True)
            cols = slice(2 * bank * DS, 2 * (bank + 1) * DS)
            nc.vector.tensor_tensor(
                out=diff[:, cols], in0=hh[:].rearrange("b i d -> b (i d)"), in1=h_sb[:, cols], op=SUBTRACT
            )

        w_codes = keep.tile([P, GROUPS, PASSES * P], U32, align_bytes=64)
        w_scales = keep.tile([P, GROUPS, PASSES * P], U8, align_bytes=64)
        z = keep.tile([P, D], F32)
        g = keep.tile([P, D], F32)
        blend = keep.tile([P, D], F32)
        result = keep.tile([P, D], F32)

        def quantise_group(grp):
            w_words = w_sb[grp][:].bitcast(F32)
            w_flip = flip.tile([P, PASSES, HALVES, P], F32, tag="flip", name="w_flip")
            for c in range(PASSES):
                for u in range(HALVES):
                    first = (c * HALVES + u) * P
                    nc.tensor.transpose(w_flip[:, c, u, :], w_words[:, first : first + P], ident_f32[:])
            w_grouped = stage.tile([P, PASSES, P, PACK], BF16, align_bytes=64, name="w_grouped")
            nc.scalar.copy(out=w_grouped[:].bitcast(F32), in_=w_flip[:].rearrange("p c u o -> p c o u"))
            nc.vector.quantize_mx(
                out=w_codes[:, grp, :].bitcast(FP8X4),
                scales=w_scales[:, grp, :],
                in_=w_grouped[:].rearrange("p c o t -> p (c o t)"),
            )

        def multiply_group(grp):
            cols = slice(grp * P, (grp + 1) * P)
            h2g = gate.tile([P, P], F32, name="h2g")
            for c in range(PASSES):
                nc.tensor.matmul_mx(
                    out=h2g[:],
                    lhsT=h_codes[:, c * P : (c + 1) * P].bitcast(FP8X4),
                    lhsT_scale=h_scales[:, c * P : (c + 1) * P],
                    rhs=w_codes[:, grp, c * P : (c + 1) * P].bitcast(FP8X4),
                    rhs_scale=w_scales[:, grp, c * P : (c + 1) * P],
                    start=(c == 0),
                    stop=(c == PASSES - 1),
                )
            nc.vector.tensor_tensor(out=z[:, cols], in0=h2g[:], in1=pre[:, cols], op=ADD)

        def blend_group(grp):
            cols = slice(grp * P, (grp + 1) * P)
            nc.scalar.activation(out=g[:, cols], in_=z[:, cols], func=SIGMOID)
            nc.vector.tensor_tensor(out=blend[:, cols], in0=g[:, cols], in1=diff[:, cols], op=MULT)
            nc.vector.tensor_tensor(out=result[:, cols], in0=blend[:, cols], in1=h_sb[:, cols], op=ADD)
            nc.sync.dma_start(out=out[:, cols], in_=result[:, cols])

        for rnd in range(ROUNDS + BLEND_LAG):
            for i in range(RUN):
                if rnd < ROUNDS:
                    quantise_group(rnd * RUN + i)
            for i in range(RUN):
                if 0 <= rnd - MULTIPLY_LAG < ROUNDS:
                    multiply_group((rnd - MULTIPLY_LAG) * RUN + i)
            for i in range(RUN):
                if 0 <= rnd - BLEND_LAG:
                    blend_group((rnd - BLEND_LAG) * RUN + i)
